import numpy as np
import ml_dtypes


def mxq(x, axis, fmt="e4m3"):
    dtype, down = {"e4m3": (ml_dtypes.float8_e4m3fn, 7), "e5m2": (ml_dtypes.float8_e5m2, 14)}[fmt]
    v = np.moveaxis(np.asarray(x, np.float32).astype(ml_dtypes.bfloat16).astype(np.float64), axis, -1)
    blocks = v.reshape(v.shape[:-1] + (-1, 32))
    amax = np.abs(blocks).max(-1, keepdims=True)
    byte = np.maximum(np.where(amax > 0, np.frexp(amax)[1] - 1 + 127, 0) - down, 1)
    scale = np.exp2(byte - 127.0)
    codes = (blocks / scale).astype(np.float32).astype(dtype).astype(np.float64)
    return np.moveaxis((codes * scale).reshape(v.shape), -1, axis)


WIDE = False


def mx_kscale(k):
    if not WIDE:
        return np.ones(k)
    levels = np.array([10, -10, 5, -5, 0])
    if k % 512:
        return np.exp2(np.random.permutation(np.resize(levels, k // 32))).repeat(32)
    a = np.empty((k // 512, 16))
    for p in range(k // 512):
        a[p, :8] = np.random.permutation(np.resize(levels, 8))
        for g in range(8):
            far = levels[np.abs(levels - a[p, g]) >= 10]
            a[p, g + 8] = far[np.random.randint(len(far))]
    return np.exp2(a.ravel()).repeat(32)


BF16 = ml_dtypes.bfloat16


def bf(x):
    return np.asarray(x, np.float32).astype(BF16)


def f64(x):
    return np.asarray(x).astype(np.float64)


N, NFEAT, NHEADS, NHID, NCLASS = 4096, 512, 4, 32, 128
P = 0.08


def elu(v):
    return np.where(v > 0, v, np.exp(np.minimum(v, 0.0)) - 1.0)


def setup_inputs():
    s, t = mx_kscale(NFEAT), mx_kscale(N)
    edges = np.random.random((N, N)) < P
    return {"x": bf(np.random.standard_normal((N, NFEAT)) * s / t[:, None]),
            "adj": bf(edges * (0.5 + np.random.random((N, N))) * t),
            "W0": bf(np.random.standard_normal((NHEADS, NFEAT, NHID)) * 1.5 / np.sqrt(NFEAT * P * N) / s[:, None])}


def reference(x, adj, W0):
    h = mxq(f64(x), 1, "e4m3") @ mxq(f64(W0), 1, "e4m3")
    hp = mxq(f64(adj), 1, "e4m3") @ mxq(h, 1, "e4m3")
    return elu(hp).transpose(1, 0, 2).reshape(N, NHEADS * NHID)

@@ -1,0 +1,242 @@
+from contextlib import ExitStack
+
+import concourse.mybir as mybir
+from concourse.masks import make_identity
+
+BF16 = mybir.dt.bfloat16
+F32 = mybir.dt.float32
+U32 = mybir.dt.uint32
+U8 = mybir.dt.uint8
+FP8X4 = mybir.dt.float8_e4m3fn_x4
+ACT = mybir.ActivationFunctionType
+ALU = mybir.AluOpType
+
+P = 128
+PACK = 4
+K_PASS = P * PACK
+
+NODES = 4096
+FEATURES = 512
+HEADS = 4
+HIDDEN = 32
+OUT_COLS = HEADS * HIDDEN
+
+SLAB_COLS = 4096
+CHUNKS = SLAB_COLS // K_PASS
+BANK_WORDS = 512
+SLAB_BANKS = SLAB_COLS // 2 // BANK_WORDS
+BANK_CHUNKS = CHUNKS // SLAB_BANKS
+
+X_SLABS = NODES * FEATURES // (P * SLAB_COLS)
+ADJ_SLABS = NODES // P
+SLABS = X_SLABS + ADJ_SLABS
+BLOCK_SLABS = 4
+
+X_RUN = PACK * FEATURES
+ROWS_BUFS = 10
+
+FLOPS = 2 * NODES * FEATURES * OUT_COLS + 2 * NODES * NODES * OUT_COLS
+
+
+def group_of(a):
+    first = a - a % BLOCK_SLABS
+    last = first + BLOCK_SLABS - 1
+    if last == ADJ_SLABS - 1:
+        if a == last:
+            first = last
+        else:
+            last = last - 1
+    return first, last
+
+
+def tile_gat_pa_t_kernel(tc, x, adj, W0, out):
+    nc = tc.nc
+
+    x_view = x.rearrange("(j p t) f -> p j (t f)", p=P, t=PACK)
+    w_view = W0.flatten_outer_dims().rearrange("(h q t) f -> q h (t f)", q=P, t=PACK)
+
+    with ExitStack() as stack:
+        const = stack.enter_context(tc.tile_pool(name="const", bufs=1))
+        rows_pool = stack.enter_context(tc.tile_pool(name="rows", bufs=ROWS_BUFS))
+        grouped_pool = stack.enter_context(tc.tile_pool(name="grouped", bufs=3))
+        codes_pool = stack.enter_context(tc.tile_pool(name="codes", bufs=3))
+        elu_pool = stack.enter_context(tc.tile_pool(name="elu", bufs=2))
+        turned_psum = stack.enter_context(tc.psum_pool(name="turned", bufs=6))
+        sums_psum = stack.enter_context(tc.psum_pool(name="sums", bufs=2))
+        stack.enter_context(tc.manual_schedule())
+
+        rows_of = {}
+        grouped_of = {}
+        codes_of = {}
+        scales_of = {}
+        sums_of = {}
+        exp_of = {}
+
+        def load(s):
+            rows = rows_pool.tile([P, SLAB_COLS], BF16)
+            rows_of[s] = rows
+            pieces = SLAB_BANKS if s == 0 or s == SLABS - 1 else 1
+            width = SLAB_COLS // pieces
+            for piece in range(pieces):
+                cols = slice(piece * width, (piece + 1) * width)
+                if s < X_SLABS:
+                    run, start = divmod(s * SLAB_COLS + piece * width, X_RUN)
+                    run_width = min(width, X_RUN)
+                    nc.sync.dma_start(
+                        out=rows[:, cols].rearrange("p (j c) -> p j c", c=run_width),
+                        in_=x_view[:, run : run + width // run_width, start : start + run_width],
+                    )
+                else:
+                    block, i = divmod(s - X_SLABS, BLOCK_SLABS)
+                    block_rows = adj[block * BLOCK_SLABS * P : (block + 1) * BLOCK_SLABS * P, :]
+                    slab_rows = block_rows.rearrange("(p i) k -> p i k", i=BLOCK_SLABS)[:, i, :]
+                    nc.sync.dma_start(out=rows[:, cols], in_=slab_rows[:, cols])
+
+        def turn(s):
+            words = rows_of[s][:].bitcast(F32)
+            grouped = grouped_pool.tile([P, SLAB_COLS], BF16, align_bytes=64)
+            grouped_of[s] = grouped
+            grouped_words = grouped[:].bitcast(F32)
+            for b in range(SLAB_BANKS):
+                turned = turned_psum.tile([P, 2 * BANK_CHUNKS, P], F32)
+                for j in range(2 * BANK_CHUNKS):
+                    first = (b * BANK_CHUNKS + j // 2) * 2 * P + j % 2
+                    nc.tensor.transpose(
+                        turned[:, j, :], words[:, first : first + 2 * P - 1 : 2], ident[:]
+                    )
+                copy = nc.vector.tensor_copy if b == 0 else nc.scalar.copy
+                copy(
+                    out=grouped_words[:, b * BANK_WORDS : (b + 1) * BANK_WORDS].rearrange(
+                        "p (c r u) -> p c r u", c=BANK_CHUNKS, u=2
+                    ),
+                    in_=turned[:].rearrange("p (c u) r -> p c r u", u=2),
+                )
+
+        def quantise(s):
+            codes = codes_pool.tile([P, CHUNKS * P], U32, align_bytes=64)
+            scales = codes_pool.tile([P, CHUNKS * P], U8, align_bytes=64)
+            codes_of[s] = codes
+            scales_of[s] = scales
+            nc.vector.quantize_mx(
+                out=codes[:].bitcast(FP8X4), scales=scales[:], in_=grouped_of[s][:]
+            )
+
+        def mx_pass(s, c, acc, rhs_codes, rhs_scales, start, stop):
+            cols = slice(c * P, (c + 1) * P)
+            nc.tensor.matmul_mx(
+                out=acc,
+                lhsT=codes_of[s][:, cols].bitcast(FP8X4),
+                lhsT_scale=scales_of[s][:, cols],
+                rhs=rhs_codes.bitcast(FP8X4),
+                rhs_scale=rhs_scales,
+                start=start,
+                stop=stop,
+            )
+
+        def project(s):
+            for half in range(2):
+                g_sums = sums_psum.tile([P, PACK, OUT_COLS], F32, tag="sums")
+                for t in range(PACK):
+                    mx_pass(s, PACK * half + t, g_sums[:, t, :], w_codes[:], w_scales[:], True, True)
+                copy = nc.vector.tensor_copy if half == 0 else nc.scalar.copy
+                copy(out=g_grouped[:, 2 * s + half, :, :], in_=g_sums[:].rearrange("p t c -> p c t"))
+            cols = slice(2 * s * OUT_COLS, (2 * s + 2) * OUT_COLS)
+            nc.vector.quantize_mx(
+                out=g_codes[:, cols].bitcast(FP8X4),
+                scales=g_scales[:, cols],
+                in_=g_grouped[:, 2 * s : 2 * s + 2, :, :].rearrange("p g c t -> p (g c t)"),
+            )
+
+        def aggregate(a):
+            first, last = group_of(a)
+            if a == first:
+                sums = sums_psum.tile([P, BLOCK_SLABS, OUT_COLS], F32, tag="sums")
+                sums_of[first] = sums
+            acc = sums_of[first][:, a - first, :]
+            for c in range(CHUNKS):
+                cols = slice(c * OUT_COLS, (c + 1) * OUT_COLS)
+                mx_pass(
+                    X_SLABS + a, c, acc, g_codes[:, cols], g_scales[:, cols], c == 0, c == CHUNKS - 1
+                )
+            if a == last:
+                width = (last - first + 1) * OUT_COLS
+                v = sums_of[first][:].rearrange("p i c -> p (i c)")[:, 0:width]
+                minus_min = elu_pool.tile([P, BLOCK_SLABS * OUT_COLS], F32)
+                nc.scalar.activation(out=minus_min[:, 0:width], in_=v, func=ACT.Relu, scale=-1.0)
+                exp_min = elu_pool.tile([P, BLOCK_SLABS * OUT_COLS], F32)
+                nc.scalar.activation(
+                    out=exp_min[:, 0:width], in_=minus_min[:, 0:width], func=ACT.Exp, scale=-1.0
+                )
+                exp_of[first] = exp_min
+
+        def result_cols(first, last):
+            return slice(first * OUT_COLS, (last + 1) * OUT_COLS)
+
+        def finish(a):
+            first, last = group_of(a)
+            if a == last:
+                width = (last - first + 1) * OUT_COLS
+                nc.vector.scalar_tensor_tensor(
+                    out=results[:, result_cols(first, last)],
+                    in0=exp_of[first][:, 0:width],
+                    scalar=-1.0,
+                    in1=sums_of[first][:].rearrange("p i c -> p (i c)")[:, 0:width],
+                    op0=ALU.add,
+                    op1=ALU.max,
+                )
+
+        def store(a):
+            first, last = group_of(a)
+            if a == last:
+                block = first // BLOCK_SLABS
+                block_out = out[block * BLOCK_SLABS * P : (block + 1) * BLOCK_SLABS * P, :]
+                in_block = slice(
+                    (first - block * BLOCK_SLABS) * OUT_COLS, (last + 1 - block * BLOCK_SLABS) * OUT_COLS
+                )
+                nc.sync.dma_start(
+                    out=block_out.rearrange("(p i) c -> p (i c)", i=BLOCK_SLABS)[:, in_block],
+                    in_=results[:, result_cols(first, last)],
+                )
+
+        w_raw = const.tile([P, HEADS, PACK * HIDDEN], BF16)
+        nc.scalar.dma_start(out=w_raw[:], in_=w_view)
+        for s in range(ROWS_BUFS):
+            load(s)
+        ident = const.tile([P, P], F32)
+        make_identity(nc, ident[:])
+        table_warmer = const.tile([P, 1], F32)
+        nc.scalar.activation(out=table_warmer[:], in_=ident[:, 0:1], func=ACT.Exp)
+        w_grouped = const.tile([P, OUT_COLS, PACK], BF16, align_bytes=64)
+        for h in range(HEADS):
+            nc.vector.tensor_copy(
+                out=w_grouped[:, HIDDEN * h : HIDDEN * (h + 1), :],
+                in_=w_raw[:, h, :].rearrange("q (t f) -> q f t", t=PACK),
+            )
+        w_codes = const.tile([P, OUT_COLS], U32, align_bytes=64)
+        w_scales = const.tile([P, OUT_COLS], U8, align_bytes=64)
+        nc.vector.quantize_mx(
+            out=w_codes[:].bitcast(FP8X4),
+            scales=w_scales[:],
+            in_=w_grouped[:].rearrange("q c t -> q (c t)"),
+        )
+        g_grouped = const.tile([P, CHUNKS, OUT_COLS, PACK], BF16, align_bytes=64)
+        g_codes = const.tile([P, CHUNKS * OUT_COLS], U32, align_bytes=64)
+        g_scales = const.tile([P, CHUNKS * OUT_COLS], U8, align_bytes=64)
+        results = const.tile([P, ADJ_SLABS * OUT_COLS], F32)
+
+        for step in range(SLABS + 3):
+            if step < SLABS:
+                turn(step)
+                if step + ROWS_BUFS < SLABS:
+                    load(step + ROWS_BUFS)
+            if 0 <= step - 1 < SLABS:
+                quantise(step - 1)
+            if X_SLABS <= step - 3 < SLABS:
+                finish(step - 3 - X_SLABS)
+            if 0 <= step - 2 < X_SLABS:
+                project(step - 2)
+            if X_SLABS <= step - 2 < SLABS:
+                aggregate(step - 2 - X_SLABS)
+
+        for a in range(ADJ_SLABS):
+            store(a)

@@ -34,6 +34,8 @@ BLOCK_SLABS = 4
 
 X_RUN = PACK * FEATURES
 ROWS_BUFS = 10
+SPLIT_BANKS = 3
+PLAIN_BANKS = SLAB_BANKS - SPLIT_BANKS
 
 FLOPS = 2 * NODES * FEATURES * OUT_COLS + 2 * NODES * NODES * OUT_COLS
 
@@ -58,6 +60,7 @@ def tile_gat_pa_t_kernel(tc, x, adj, W0, out):
     with ExitStack() as stack:
         const = stack.enter_context(tc.tile_pool(name="const", bufs=1))
         rows_pool = stack.enter_context(tc.tile_pool(name="rows", bufs=ROWS_BUFS))
+        halves_pool = stack.enter_context(tc.tile_pool(name="halves", bufs=3))
         grouped_pool = stack.enter_context(tc.tile_pool(name="grouped", bufs=3))
         codes_pool = stack.enter_context(tc.tile_pool(name="codes", bufs=3))
         elu_pool = stack.enter_context(tc.tile_pool(name="elu", bufs=2))
@@ -66,6 +69,7 @@ def tile_gat_pa_t_kernel(tc, x, adj, W0, out):
         stack.enter_context(tc.manual_schedule())
 
         rows_of = {}
+        halves_of = {}
         grouped_of = {}
         codes_of = {}
         scales_of = {}
@@ -92,6 +96,20 @@ def tile_gat_pa_t_kernel(tc, x, adj, W0, out):
                     slab_rows = block_rows.rearrange("(p i) k -> p i k", i=BLOCK_SLABS)[:, i, :]
                     nc.sync.dma_start(out=rows[:, cols], in_=slab_rows[:, cols])
 
+        def plain_banks(s):
+            return SLAB_BANKS if s == 0 else PLAIN_BANKS
+
+        def split(s):
+            if plain_banks(s) == SLAB_BANKS:
+                return
+            words = rows_of[s][:].bitcast(F32)
+            halves = halves_pool.tile([P, SPLIT_BANKS * BANK_WORDS], F32)
+            halves_of[s] = halves
+            nc.vector.tensor_copy(
+                out=halves[:].rearrange("r (c u p) -> r c u p", u=2, p=P),
+                in_=words[:, PLAIN_BANKS * BANK_WORDS :].rearrange("r (c p u) -> r c u p", u=2, p=P),
+            )
+
         def turn(s):
             words = rows_of[s][:].bitcast(F32)
             grouped = grouped_pool.tile([P, SLAB_COLS], BF16, align_bytes=64)
@@ -100,11 +118,14 @@ def tile_gat_pa_t_kernel(tc, x, adj, W0, out):
             for b in range(SLAB_BANKS):
                 turned = turned_psum.tile([P, 2 * BANK_CHUNKS, P], F32)
                 for j in range(2 * BANK_CHUNKS):
-                    first = (b * BANK_CHUNKS + j // 2) * 2 * P + j % 2
-                    nc.tensor.transpose(
-                        turned[:, j, :], words[:, first : first + 2 * P - 1 : 2], ident[:]
-                    )
-                copy = nc.vector.tensor_copy if b == 0 else nc.scalar.copy
+                    if b < plain_banks(s):
+                        first = (b * BANK_CHUNKS + j // 2) * 2 * P + j % 2
+                        operand = words[:, first : first + 2 * P - 1 : 2]
+                    else:
+                        first = (b - PLAIN_BANKS) * BANK_WORDS + j * P
+                        operand = halves_of[s][:, first : first + P]
+                    nc.tensor.transpose(turned[:, j, :], operand, ident[:])
+                copy = nc.vector.tensor_copy if b == 0 and s % 2 == 0 else nc.scalar.copy
                 copy(
                     out=grouped_words[:, b * BANK_WORDS : (b + 1) * BANK_WORDS].rearrange(
                         "p (c r u) -> p c r u", c=BANK_CHUNKS, u=2
@@ -225,12 +246,14 @@ def tile_gat_pa_t_kernel(tc, x, adj, W0, out):
         results = const.tile([P, ADJ_SLABS * OUT_COLS], F32)
 
         for step in range(SLABS + 3):
+            if 0 <= step - 1 < SLABS:
+                quantise(step - 1)
             if step < SLABS:
                 turn(step)
                 if step + ROWS_BUFS < SLABS:
                     load(step + ROWS_BUFS)
-            if 0 <= step - 1 < SLABS:
-                quantise(step - 1)
+            if step + 1 < SLABS:
+                split(step + 1)
             if X_SLABS <= step - 3 < SLABS:
                 finish(step - 3 - X_SLABS)
             if 0 <= step - 2 < X_SLABS:

@@ -34,7 +34,8 @@ BLOCK_SLABS = 4
 
 X_RUN = PACK * FEATURES
 ROWS_BUFS = 10
-SPLIT_BANKS = 3
+SPLIT_BANKS = 2
+LINE_WORDS = 4
 PLAIN_BANKS = SLAB_BANKS - SPLIT_BANKS
 
 FLOPS = 2 * NODES * FEATURES * OUT_COLS + 2 * NODES * NODES * OUT_COLS
@@ -106,8 +107,10 @@ def tile_gat_pa_t_kernel(tc, x, adj, W0, out):
             halves = halves_pool.tile([P, SPLIT_BANKS * BANK_WORDS], F32)
             halves_of[s] = halves
             nc.vector.tensor_copy(
-                out=halves[:].rearrange("r (c u p) -> r c u p", u=2, p=P),
-                in_=words[:, PLAIN_BANKS * BANK_WORDS :].rearrange("r (c p u) -> r c u p", u=2, p=P),
+                out=halves[:].rearrange("r (u m i) -> r m u i", u=2, i=LINE_WORDS),
+                in_=words[:, PLAIN_BANKS * BANK_WORDS :].rearrange(
+                    "r (m i u) -> r m u i", u=2, i=LINE_WORDS
+                ),
             )
 
         def turn(s):
@@ -122,10 +125,10 @@ def tile_gat_pa_t_kernel(tc, x, adj, W0, out):
                         first = (b * BANK_CHUNKS + j // 2) * 2 * P + j % 2
                         operand = words[:, first : first + 2 * P - 1 : 2]
                     else:
-                        first = (b - PLAIN_BANKS) * BANK_WORDS + j * P
+                        first = (j % 2 * SPLIT_BANKS + b - PLAIN_BANKS) * BANK_CHUNKS * P + j // 2 * P
                         operand = halves_of[s][:, first : first + P]
                     nc.tensor.transpose(turned[:, j, :], operand, ident[:])
-                copy = nc.vector.tensor_copy if b == 0 and s % 2 == 0 else nc.scalar.copy
+                copy = nc.vector.tensor_copy if b == 0 and s % 4 == 0 else nc.scalar.copy
                 copy(
                     out=grouped_words[:, b * BANK_WORDS : (b + 1) * BANK_WORDS].rearrange(
                         "p (c r u) -> p c r u", c=BANK_CHUNKS, u=2
@@ -133,13 +136,17 @@ def tile_gat_pa_t_kernel(tc, x, adj, W0, out):
                     in_=turned[:].rearrange("p (c u) r -> p c r u", u=2),
                 )
 
-        def quantise(s):
-            codes = codes_pool.tile([P, CHUNKS * P], U32, align_bytes=64)
-            scales = codes_pool.tile([P, CHUNKS * P], U8, align_bytes=64)
-            codes_of[s] = codes
-            scales_of[s] = scales
+        def quantise(s, half):
+            if half == 0:
+                codes = codes_pool.tile([P, CHUNKS * P], U32, align_bytes=64)
+                scales = codes_pool.tile([P, CHUNKS * P], U8, align_bytes=64)
+                codes_of[s] = codes
+                scales_of[s] = scales
+            words = slice(half * CHUNKS // 2 * P, (half + 1) * CHUNKS // 2 * P)
             nc.vector.quantize_mx(
-                out=codes[:].bitcast(FP8X4), scales=scales[:], in_=grouped_of[s][:]
+                out=codes_of[s][:, words].bitcast(FP8X4),
+                scales=scales_of[s][:, words],
+                in_=grouped_of[s][:, PACK * words.start : PACK * words.stop],
             )
 
         def mx_pass(s, c, acc, rhs_codes, rhs_scales, start, stop):
@@ -247,13 +254,15 @@ def tile_gat_pa_t_kernel(tc, x, adj, W0, out):
 
         for step in range(SLABS + 3):
             if 0 <= step - 1 < SLABS:
-                quantise(step - 1)
+                quantise(step - 1, 0)
+            if step + 1 < SLABS:
+                split(step + 1)
             if step < SLABS:
                 turn(step)
                 if step + ROWS_BUFS < SLABS:
                     load(step + ROWS_BUFS)
-            if step + 1 < SLABS:
-                split(step + 1)
+            if 0 <= step - 1 < SLABS:
+                quantise(step - 1, 1)
             if X_SLABS <= step - 3 < SLABS:
                 finish(step - 3 - X_SLABS)
             if 0 <= step - 2 < X_SLABS:

@@ -80,7 +80,7 @@ def tile_gat_pa_t_kernel(tc, x, adj, W0, out):
         def load(s):
             rows = rows_pool.tile([P, SLAB_COLS], BF16)
             rows_of[s] = rows
-            pieces = SLAB_BANKS if s == 0 or s == SLABS - 1 else 1
+            pieces = SLAB_BANKS if s < X_SLABS or s == SLABS - 1 else 1
             width = SLAB_COLS // pieces
             for piece in range(pieces):
                 cols = slice(piece * width, (piece + 1) * width)
@@ -98,7 +98,7 @@ def tile_gat_pa_t_kernel(tc, x, adj, W0, out):
                     nc.sync.dma_start(out=rows[:, cols], in_=slab_rows[:, cols])
 
         def plain_banks(s):
-            return SLAB_BANKS if s == 0 else PLAIN_BANKS
+            return SLAB_BANKS if s < X_SLABS else PLAIN_BANKS
 
         def split(s):
             if plain_banks(s) == SLAB_BANKS:
@@ -128,7 +128,7 @@ def tile_gat_pa_t_kernel(tc, x, adj, W0, out):
                         first = (j % 2 * SPLIT_BANKS + b - PLAIN_BANKS) * BANK_CHUNKS * P + j // 2 * P
                         operand = halves_of[s][:, first : first + P]
                     nc.tensor.transpose(turned[:, j, :], operand, ident[:])
-                copy = nc.vector.tensor_copy if b == 0 and s % 4 == 0 else nc.scalar.copy
+                copy = nc.vector.tensor_copy if b == 1 and s % 4 == 3 else nc.scalar.copy
                 copy(
                     out=grouped_words[:, b * BANK_WORDS : (b + 1) * BANK_WORDS].rearrange(
                         "p (c r u) -> p c r u", c=BANK_CHUNKS, u=2

@@ -75,6 +75,7 @@ def tile_gat_pa_t_kernel(tc, x, adj, W0, out):
         codes_of = {}
         scales_of = {}
         sums_of = {}
+        minus_min_of = {}
         exp_of = {}
 
         def load(s):
@@ -113,7 +114,7 @@ def tile_gat_pa_t_kernel(tc, x, adj, W0, out):
                 ),
             )
 
-        def turn(s):
+        def turn(s, passes):
             words = rows_of[s][:].bitcast(F32)
             grouped = grouped_pool.tile([P, SLAB_COLS], BF16, align_bytes=64)
             grouped_of[s] = grouped
@@ -128,13 +129,15 @@ def tile_gat_pa_t_kernel(tc, x, adj, W0, out):
                         first = (j % 2 * SPLIT_BANKS + b - PLAIN_BANKS) * BANK_CHUNKS * P + j // 2 * P
                         operand = halves_of[s][:, first : first + P]
                     nc.tensor.transpose(turned[:, j, :], operand, ident[:])
-                copy = nc.vector.tensor_copy if b == 1 and s % 4 == 3 else nc.scalar.copy
+                copy = nc.vector.tensor_copy if b == 2 and s % 4 == 2 else nc.scalar.copy
                 copy(
                     out=grouped_words[:, b * BANK_WORDS : (b + 1) * BANK_WORDS].rearrange(
                         "p (c r u) -> p c r u", c=BANK_CHUNKS, u=2
                     ),
                     in_=turned[:].rearrange("p (c u) r -> p c r u", u=2),
                 )
+                if b < len(passes):
+                    passes[b]()
 
         def quantise(s, half):
             if half == 0:
@@ -186,16 +189,34 @@ def tile_gat_pa_t_kernel(tc, x, adj, W0, out):
                 mx_pass(
                     X_SLABS + a, c, acc, g_codes[:, cols], g_scales[:, cols], c == 0, c == CHUNKS - 1
                 )
-            if a == last:
-                width = (last - first + 1) * OUT_COLS
-                v = sums_of[first][:].rearrange("p i c -> p (i c)")[:, 0:width]
-                minus_min = elu_pool.tile([P, BLOCK_SLABS * OUT_COLS], F32)
-                nc.scalar.activation(out=minus_min[:, 0:width], in_=v, func=ACT.Relu, scale=-1.0)
-                exp_min = elu_pool.tile([P, BLOCK_SLABS * OUT_COLS], F32)
-                nc.scalar.activation(
-                    out=exp_min[:, 0:width], in_=minus_min[:, 0:width], func=ACT.Exp, scale=-1.0
-                )
-                exp_of[first] = exp_min
+
+        def clamp(first, last):
+            width = (last - first + 1) * OUT_COLS
+            minus_min = elu_pool.tile([P, BLOCK_SLABS * OUT_COLS], F32)
+            minus_min_of[first] = minus_min
+            nc.scalar.activation(
+                out=minus_min[:, 0:width],
+                in_=sums_of[first][:].rearrange("p i c -> p (i c)")[:, 0:width],
+                func=ACT.Relu,
+                scale=-1.0,
+            )
+
+        def exponentiate(first, last):
+            width = (last - first + 1) * OUT_COLS
+            exp_min = elu_pool.tile([P, BLOCK_SLABS * OUT_COLS], F32)
+            exp_of[first] = exp_min
+            nc.scalar.activation(
+                out=exp_min[:, 0:width],
+                in_=minus_min_of[first][:, 0:width],
+                func=ACT.Exp,
+                scale=-1.0,
+            )
+
+        def elu_passes(s):
+            if not X_SLABS <= s < SLABS or group_of(s - X_SLABS)[1] != s - X_SLABS:
+                return []
+            first, last = group_of(s - X_SLABS)
+            return [lambda: clamp(first, last), lambda: exponentiate(first, last)]
 
         def result_cols(first, last):
             return slice(first * OUT_COLS, (last + 1) * OUT_COLS)
@@ -257,14 +278,18 @@ def tile_gat_pa_t_kernel(tc, x, adj, W0, out):
                 quantise(step - 1, 0)
             if step + 1 < SLABS:
                 split(step + 1)
-            if step < SLABS:
-                turn(step)
-                if step + ROWS_BUFS < SLABS:
-                    load(step + ROWS_BUFS)
             if 0 <= step - 1 < SLABS:
                 quantise(step - 1, 1)
-            if X_SLABS <= step - 3 < SLABS:
-                finish(step - 3 - X_SLABS)
+            if step < SLABS:
+                turn(step, elu_passes(step - 3))
+                if step + ROWS_BUFS < SLABS:
+                    load(step + ROWS_BUFS)
+            else:
+                for elu_pass in elu_passes(step - 3):
+                    elu_pass()
+            s = step - 4 if step < SLABS else step - 3
+            if X_SLABS <= s < SLABS:
+                finish(s - X_SLABS)
             if 0 <= step - 2 < X_SLABS:
                 project(step - 2)
             if X_SLABS <= step - 2 < SLABS:

@@ -34,9 +34,8 @@ BLOCK_SLABS = 4
 
 X_RUN = PACK * FEATURES
 ROWS_BUFS = 10
-SPLIT_BANKS = 2
+PLAIN_BANKS = 2
 LINE_WORDS = 4
-PLAIN_BANKS = SLAB_BANKS - SPLIT_BANKS
 
 FLOPS = 2 * NODES * FEATURES * OUT_COLS + 2 * NODES * NODES * OUT_COLS
 
@@ -99,17 +98,20 @@ def tile_gat_pa_t_kernel(tc, x, adj, W0, out):
                     nc.sync.dma_start(out=rows[:, cols], in_=slab_rows[:, cols])
 
         def plain_banks(s):
-            return SLAB_BANKS if s < X_SLABS else PLAIN_BANKS
+            if s < X_SLABS:
+                return SLAB_BANKS
+            return PLAIN_BANKS - 1 if s % 4 == 1 else PLAIN_BANKS
 
         def split(s):
-            if plain_banks(s) == SLAB_BANKS:
+            plain = plain_banks(s)
+            if plain == SLAB_BANKS:
                 return
             words = rows_of[s][:].bitcast(F32)
-            halves = halves_pool.tile([P, SPLIT_BANKS * BANK_WORDS], F32)
+            halves = halves_pool.tile([P, (SLAB_BANKS - plain) * BANK_WORDS], F32)
             halves_of[s] = halves
             nc.vector.tensor_copy(
                 out=halves[:].rearrange("r (u m i) -> r m u i", u=2, i=LINE_WORDS),
-                in_=words[:, PLAIN_BANKS * BANK_WORDS :].rearrange(
+                in_=words[:, plain * BANK_WORDS :].rearrange(
                     "r (m i u) -> r m u i", u=2, i=LINE_WORDS
                 ),
             )
@@ -119,14 +121,15 @@ def tile_gat_pa_t_kernel(tc, x, adj, W0, out):
             grouped = grouped_pool.tile([P, SLAB_COLS], BF16, align_bytes=64)
             grouped_of[s] = grouped
             grouped_words = grouped[:].bitcast(F32)
+            plain = plain_banks(s)
             for b in range(SLAB_BANKS):
                 turned = turned_psum.tile([P, 2 * BANK_CHUNKS, P], F32)
                 for j in range(2 * BANK_CHUNKS):
-                    if b < plain_banks(s):
+                    if b < plain:
                         first = (b * BANK_CHUNKS + j // 2) * 2 * P + j % 2
                         operand = words[:, first : first + 2 * P - 1 : 2]
                     else:
-                        first = (j % 2 * SPLIT_BANKS + b - PLAIN_BANKS) * BANK_CHUNKS * P + j // 2 * P
+                        first = (j % 2 * (SLAB_BANKS - plain) + b - plain) * BANK_CHUNKS * P + j // 2 * P
                         operand = halves_of[s][:, first : first + P]
                     nc.tensor.transpose(turned[:, j, :], operand, ident[:])
                 copy = nc.vector.tensor_copy if b == 2 and s % 4 == 2 else nc.scalar.copy
@@ -139,13 +142,13 @@ def tile_gat_pa_t_kernel(tc, x, adj, W0, out):
                 if b < len(passes):
                     passes[b]()
 
-        def quantise(s, half):
-            if half == 0:
+        def quantise(s, part, parts):
+            if part == 0:
                 codes = codes_pool.tile([P, CHUNKS * P], U32, align_bytes=64)
                 scales = codes_pool.tile([P, CHUNKS * P], U8, align_bytes=64)
                 codes_of[s] = codes
                 scales_of[s] = scales
-            words = slice(half * CHUNKS // 2 * P, (half + 1) * CHUNKS // 2 * P)
+            words = slice(part * CHUNKS // parts * P, (part + 1) * CHUNKS // parts * P)
             nc.vector.quantize_mx(
                 out=codes_of[s][:, words].bitcast(FP8X4),
                 scales=scales_of[s][:, words],
@@ -274,12 +277,14 @@ def tile_gat_pa_t_kernel(tc, x, adj, W0, out):
         results = const.tile([P, ADJ_SLABS * OUT_COLS], F32)
 
         for step in range(SLABS + 3):
+            parts = SLAB_BANKS if step == SLABS else 2
             if 0 <= step - 1 < SLABS:
-                quantise(step - 1, 0)
+                quantise(step - 1, 0, parts)
             if step + 1 < SLABS:
                 split(step + 1)
             if 0 <= step - 1 < SLABS:
-                quantise(step - 1, 1)
+                for part in range(1, parts):
+                    quantise(step - 1, part, parts)
             if step < SLABS:
                 turn(step, elu_passes(step - 3))
                 if step + ROWS_BUFS < SLABS:

from contextlib import ExitStack

import concourse.mybir as mybir
from concourse.masks import make_identity

BF16 = mybir.dt.bfloat16
F32 = mybir.dt.float32
U32 = mybir.dt.uint32
U8 = mybir.dt.uint8
FP8X4 = mybir.dt.float8_e4m3fn_x4
ACT = mybir.ActivationFunctionType
ALU = mybir.AluOpType

P = 128
PACK = 4
K_PASS = P * PACK

NODES = 4096
FEATURES = 512
HEADS = 4
HIDDEN = 32
OUT_COLS = HEADS * HIDDEN

SLAB_COLS = 4096
CHUNKS = SLAB_COLS // K_PASS
BANK_WORDS = 512
SLAB_BANKS = SLAB_COLS // 2 // BANK_WORDS
BANK_CHUNKS = CHUNKS // SLAB_BANKS

X_SLABS = NODES * FEATURES // (P * SLAB_COLS)
ADJ_SLABS = NODES // P
SLABS = X_SLABS + ADJ_SLABS
BLOCK_SLABS = 4

X_RUN = PACK * FEATURES
ROWS_BUFS = 10
PLAIN_BANKS = 2
LINE_WORDS = 4

FLOPS = 2 * NODES * FEATURES * OUT_COLS + 2 * NODES * NODES * OUT_COLS


def group_of(a):
    first = a - a % BLOCK_SLABS
    last = first + BLOCK_SLABS - 1
    if last == ADJ_SLABS - 1:
        if a == last:
            first = last
        else:
            last = last - 1
    return first, last


def tile_gat_pa_t_kernel(tc, x, adj, W0, out):
    nc = tc.nc

    x_view = x.rearrange("(j p t) f -> p j (t f)", p=P, t=PACK)
    w_view = W0.flatten_outer_dims().rearrange("(h q t) f -> q h (t f)", q=P, t=PACK)

    with ExitStack() as stack:
        const = stack.enter_context(tc.tile_pool(name="const", bufs=1))
        rows_pool = stack.enter_context(tc.tile_pool(name="rows", bufs=ROWS_BUFS))
        halves_pool = stack.enter_context(tc.tile_pool(name="halves", bufs=3))
        grouped_pool = stack.enter_context(tc.tile_pool(name="grouped", bufs=3))
        codes_pool = stack.enter_context(tc.tile_pool(name="codes", bufs=3))
        elu_pool = stack.enter_context(tc.tile_pool(name="elu", bufs=2))
        turned_psum = stack.enter_context(tc.psum_pool(name="turned", bufs=6))
        sums_psum = stack.enter_context(tc.psum_pool(name="sums", bufs=2))
        stack.enter_context(tc.manual_schedule())

        rows_of = {}
        halves_of = {}
        grouped_of = {}
        codes_of = {}
        scales_of = {}
        sums_of = {}
        minus_min_of = {}
        exp_of = {}

        def load(s):
            rows = rows_pool.tile([P, SLAB_COLS], BF16)
            rows_of[s] = rows
            pieces = SLAB_BANKS if s < X_SLABS or s == SLABS - 1 else 1
            width = SLAB_COLS // pieces
            for piece in range(pieces):
                cols = slice(piece * width, (piece + 1) * width)
                if s < X_SLABS:
                    run, start = divmod(s * SLAB_COLS + piece * width, X_RUN)
                    run_width = min(width, X_RUN)
                    nc.sync.dma_start(
                        out=rows[:, cols].rearrange("p (j c) -> p j c", c=run_width),
                        in_=x_view[:, run : run + width // run_width, start : start + run_width],
                    )
                else:
                    block, i = divmod(s - X_SLABS, BLOCK_SLABS)
                    block_rows = adj[block * BLOCK_SLABS * P : (block + 1) * BLOCK_SLABS * P, :]
                    slab_rows = block_rows.rearrange("(p i) k -> p i k", i=BLOCK_SLABS)[:, i, :]
                    nc.sync.dma_start(out=rows[:, cols], in_=slab_rows[:, cols])

        def plain_banks(s):
            if s < X_SLABS:
                return SLAB_BANKS
            return PLAIN_BANKS - 1 if s % 4 == 1 else PLAIN_BANKS

        def split(s):
            plain = plain_banks(s)
            if plain == SLAB_BANKS:
                return
            words = rows_of[s][:].bitcast(F32)
            halves = halves_pool.tile([P, (SLAB_BANKS - plain) * BANK_WORDS], F32)
            halves_of[s] = halves
            nc.vector.tensor_copy(
                out=halves[:].rearrange("r (u m i) -> r m u i", u=2, i=LINE_WORDS),
                in_=words[:, plain * BANK_WORDS :].rearrange(
                    "r (m i u) -> r m u i", u=2, i=LINE_WORDS
                ),
            )

        def turn(s, passes):
            words = rows_of[s][:].bitcast(F32)
            grouped = grouped_pool.tile([P, SLAB_COLS], BF16, align_bytes=64)
            grouped_of[s] = grouped
            grouped_words = grouped[:].bitcast(F32)
            plain = plain_banks(s)
            for b in range(SLAB_BANKS):
                turned = turned_psum.tile([P, 2 * BANK_CHUNKS, P], F32)
                for j in range(2 * BANK_CHUNKS):
                    if b < plain:
                        first = (b * BANK_CHUNKS + j // 2) * 2 * P + j % 2
                        operand = words[:, first : first + 2 * P - 1 : 2]
                    else:
                        first = (j % 2 * (SLAB_BANKS - plain) + b - plain) * BANK_CHUNKS * P + j // 2 * P
                        operand = halves_of[s][:, first : first + P]
                    nc.tensor.transpose(turned[:, j, :], operand, ident[:])
                copy = nc.vector.tensor_copy if b == 2 and s % 4 == 2 else nc.scalar.copy
                copy(
                    out=grouped_words[:, b * BANK_WORDS : (b + 1) * BANK_WORDS].rearrange(
                        "p (c r u) -> p c r u", c=BANK_CHUNKS, u=2
                    ),
                    in_=turned[:].rearrange("p (c u) r -> p c r u", u=2),
                )
                if b < len(passes):
                    passes[b]()

        def quantise(s, part, parts):
            if part == 0:
                codes = codes_pool.tile([P, CHUNKS * P], U32, align_bytes=64)
                scales = codes_pool.tile([P, CHUNKS * P], U8, align_bytes=64)
                codes_of[s] = codes
                scales_of[s] = scales
            words = slice(part * CHUNKS // parts * P, (part + 1) * CHUNKS // parts * P)
            nc.vector.quantize_mx(
                out=codes_of[s][:, words].bitcast(FP8X4),
                scales=scales_of[s][:, words],
                in_=grouped_of[s][:, PACK * words.start : PACK * words.stop],
            )

        def mx_pass(s, c, acc, rhs_codes, rhs_scales, start, stop):
            cols = slice(c * P, (c + 1) * P)
            nc.tensor.matmul_mx(
                out=acc,
                lhsT=codes_of[s][:, cols].bitcast(FP8X4),
                lhsT_scale=scales_of[s][:, cols],
                rhs=rhs_codes.bitcast(FP8X4),
                rhs_scale=rhs_scales,
                start=start,
                stop=stop,
            )

        def project(s):
            for half in range(2):
                g_sums = sums_psum.tile([P, PACK, OUT_COLS], F32, tag="sums")
                for t in range(PACK):
                    mx_pass(s, PACK * half + t, g_sums[:, t, :], w_codes[:], w_scales[:], True, True)
                copy = nc.vector.tensor_copy if half == 0 else nc.scalar.copy
                copy(out=g_grouped[:, 2 * s + half, :, :], in_=g_sums[:].rearrange("p t c -> p c t"))
            cols = slice(2 * s * OUT_COLS, (2 * s + 2) * OUT_COLS)
            nc.vector.quantize_mx(
                out=g_codes[:, cols].bitcast(FP8X4),
                scales=g_scales[:, cols],
                in_=g_grouped[:, 2 * s : 2 * s + 2, :, :].rearrange("p g c t -> p (g c t)"),
            )

        def aggregate(a):
            first, last = group_of(a)
            if a == first:
                sums = sums_psum.tile([P, BLOCK_SLABS, OUT_COLS], F32, tag="sums")
                sums_of[first] = sums
            acc = sums_of[first][:, a - first, :]
            for c in range(CHUNKS):
                cols = slice(c * OUT_COLS, (c + 1) * OUT_COLS)
                mx_pass(
                    X_SLABS + a, c, acc, g_codes[:, cols], g_scales[:, cols], c == 0, c == CHUNKS - 1
                )

        def clamp(first, last):
            width = (last - first + 1) * OUT_COLS
            minus_min = elu_pool.tile([P, BLOCK_SLABS * OUT_COLS], F32)
            minus_min_of[first] = minus_min
            nc.scalar.activation(
                out=minus_min[:, 0:width],
                in_=sums_of[first][:].rearrange("p i c -> p (i c)")[:, 0:width],
                func=ACT.Relu,
                scale=-1.0,
            )

        def exponentiate(first, last):
            width = (last - first + 1) * OUT_COLS
            exp_min = elu_pool.tile([P, BLOCK_SLABS * OUT_COLS], F32)
            exp_of[first] = exp_min
            nc.scalar.activation(
                out=exp_min[:, 0:width],
                in_=minus_min_of[first][:, 0:width],
                func=ACT.Exp,
                scale=-1.0,
            )

        def elu_passes(s):
            if not X_SLABS <= s < SLABS or group_of(s - X_SLABS)[1] != s - X_SLABS:
                return []
            first, last = group_of(s - X_SLABS)
            return [lambda: clamp(first, last), lambda: exponentiate(first, last)]

        def result_cols(first, last):
            return slice(first * OUT_COLS, (last + 1) * OUT_COLS)

        def finish(a):
            first, last = group_of(a)
            if a == last:
                width = (last - first + 1) * OUT_COLS
                nc.vector.scalar_tensor_tensor(
                    out=results[:, result_cols(first, last)],
                    in0=exp_of[first][:, 0:width],
                    scalar=-1.0,
                    in1=sums_of[first][:].rearrange("p i c -> p (i c)")[:, 0:width],
                    op0=ALU.add,
                    op1=ALU.max,
                )

        def store(a):
            first, last = group_of(a)
            if a == last:
                block = first // BLOCK_SLABS
                block_out = out[block * BLOCK_SLABS * P : (block + 1) * BLOCK_SLABS * P, :]
                in_block = slice(
                    (first - block * BLOCK_SLABS) * OUT_COLS, (last + 1 - block * BLOCK_SLABS) * OUT_COLS
                )
                nc.sync.dma_start(
                    out=block_out.rearrange("(p i) c -> p (i c)", i=BLOCK_SLABS)[:, in_block],
                    in_=results[:, result_cols(first, last)],
                )

        w_raw = const.tile([P, HEADS, PACK * HIDDEN], BF16)
        nc.scalar.dma_start(out=w_raw[:], in_=w_view)
        for s in range(ROWS_BUFS):
            load(s)
        ident = const.tile([P, P], F32)
        make_identity(nc, ident[:])
        table_warmer = const.tile([P, 1], F32)
        nc.scalar.activation(out=table_warmer[:], in_=ident[:, 0:1], func=ACT.Exp)
        w_grouped = const.tile([P, OUT_COLS, PACK], BF16, align_bytes=64)
        for h in range(HEADS):
            nc.vector.tensor_copy(
                out=w_grouped[:, HIDDEN * h : HIDDEN * (h + 1), :],
                in_=w_raw[:, h, :].rearrange("q (t f) -> q f t", t=PACK),
            )
        w_codes = const.tile([P, OUT_COLS], U32, align_bytes=64)
        w_scales = const.tile([P, OUT_COLS], U8, align_bytes=64)
        nc.vector.quantize_mx(
            out=w_codes[:].bitcast(FP8X4),
            scales=w_scales[:],
            in_=w_grouped[:].rearrange("q c t -> q (c t)"),
        )
        g_grouped = const.tile([P, CHUNKS, OUT_COLS, PACK], BF16, align_bytes=64)
        g_codes = const.tile([P, CHUNKS * OUT_COLS], U32, align_bytes=64)
        g_scales = const.tile([P, CHUNKS * OUT_COLS], U8, align_bytes=64)
        results = const.tile([P, ADJ_SLABS * OUT_COLS], F32)

        for step in range(SLABS + 3):
            parts = SLAB_BANKS if step == SLABS else 2
            if 0 <= step - 1 < SLABS:
                quantise(step - 1, 0, parts)
            if step + 1 < SLABS:
                split(step + 1)
            if 0 <= step - 1 < SLABS:
                for part in range(1, parts):
                    quantise(step - 1, part, parts)
            if step < SLABS:
                turn(step, elu_passes(step - 3))
                if step + ROWS_BUFS < SLABS:
                    load(step + ROWS_BUFS)
            else:
                for elu_pass in elu_passes(step - 3):
                    elu_pass()
            s = step - 4 if step < SLABS else step - 3
            if X_SLABS <= s < SLABS:
                finish(s - X_SLABS)
            if 0 <= step - 2 < X_SLABS:
                project(step - 2)
            if X_SLABS <= step - 2 < SLABS:
                aggregate(step - 2 - X_SLABS)

        for a in range(ADJ_SLABS):
            store(a)
